import numpy as np
import ml_dtypes


def mxq(x, axis, fmt="e4m3"):
    dtype, down = {"e4m3": (ml_dtypes.float8_e4m3fn, 7), "e5m2": (ml_dtypes.float8_e5m2, 14)}[fmt]
    v = np.moveaxis(np.asarray(x, np.float32).astype(ml_dtypes.bfloat16).astype(np.float64), axis, -1)
    blocks = v.reshape(v.shape[:-1] + (-1, 32))
    amax = np.abs(blocks).max(-1, keepdims=True)
    byte = np.maximum(np.where(amax > 0, np.frexp(amax)[1] - 1 + 127, 0) - down, 1)
    scale = np.exp2(byte - 127.0)
    codes = (blocks / scale).astype(np.float32).astype(dtype).astype(np.float64)
    return np.moveaxis((codes * scale).reshape(v.shape), -1, axis)


WIDE = False


def mx_kscale(k):
    if not WIDE:
        return np.ones(k)
    levels = np.array([10, -10, 5, -5, 0])
    if k % 512:
        return np.exp2(np.random.permutation(np.resize(levels, k // 32))).repeat(32)
    a = np.empty((k // 512, 16))
    for p in range(k // 512):
        a[p, :8] = np.random.permutation(np.resize(levels, 8))
        for g in range(8):
            far = levels[np.abs(levels - a[p, g]) >= 10]
            a[p, g + 8] = far[np.random.randint(len(far))]
    return np.exp2(a.ravel()).repeat(32)


BF16 = ml_dtypes.bfloat16


def bf(x):
    return np.asarray(x, np.float32).astype(BF16)


def f64(x):
    return np.asarray(x).astype(np.float64)


B, Tq, Tk, C = 2, 64, 64, 512
C2 = 2 * C
VAR_EPS = 1e-6
LN_EPS = 1e-5


def layernorm(x, g, b):
    m = x.mean(-1, keepdims=True)
    v = ((x - m) ** 2).mean(-1, keepdims=True)
    return (x - m) / np.sqrt(v + LN_EPS) * g + b


def softplus(v):
    return np.log(1.0 + np.exp(v))


def setup_inputs():
    s = mx_kscale(C)
    w = 1.0 / np.sqrt(C)
    return {"context": bf(np.random.standard_normal((B, Tk, C)) * s),
            "eps_noise": bf(np.random.standard_normal((B, Tk, C))),
            "Wk": bf(np.random.standard_normal((C2, C)) * w / s),
            "bk": bf(np.random.standard_normal(C2) * 0.2),
            "Wv": bf(np.random.standard_normal((C2, C)) * w / s),
            "bv": bf(np.random.standard_normal(C2) * 0.2),
            "ln_k_g": bf(1.0 + 0.1 * np.random.standard_normal(C)),
            "ln_k_b": bf(np.random.standard_normal(C) * 0.2),
            "ln_v_g": bf(1.0 + 0.1 * np.random.standard_normal(C)),
            "ln_v_b": bf(np.random.standard_normal(C) * 0.2)}


def reference(context, eps_noise, Wk, bk, Wv, bv, ln_k_g, ln_k_b, ln_v_g, ln_v_b):
    cq = mxq(f64(context), 2, "e4m3")
    k_out = (cq @ mxq(f64(Wk), 1, "e4m3").T) + f64(bk)
    k_mu = layernorm(k_out[..., :C], f64(ln_k_g), f64(ln_k_b))
    k_var = softplus(k_out[..., C:]) + VAR_EPS
    v_out = (cq @ mxq(f64(Wv), 1, "e4m3").T) + f64(bv)
    v_mu = layernorm(v_out[..., :C], f64(ln_v_g), f64(ln_v_b))
    v_var = softplus(v_out[..., C:]) + VAR_EPS
    v_sample = v_mu + np.sqrt(v_var) * f64(eps_noise)
    return k_mu, k_var, v_sample

@@ -1,0 +1,289 @@
+from contextlib import ExitStack
+
+import concourse.mybir as mybir
+from concourse.masks import make_identity
+
+F32 = mybir.dt.float32
+BF16 = mybir.dt.bfloat16
+U32 = mybir.dt.uint32
+U8 = mybir.dt.uint8
+FP8X4 = mybir.dt.float8_e4m3fn_x4
+ALU = mybir.AluOpType
+ACT = mybir.ActivationFunctionType
+
+P = 128
+C = 512
+BANK = 512
+PIECE = 256
+N_PIECES = 4 * C // PIECE
+V_VAR, K_VAR, V_MU, K_MU = 0, 1, 2, 3
+VAR_EPS = 1e-6
+LN_EPS = 1e-5
+
+QUANTISE_LAG = 1
+MULTIPLY_LAG = 4
+EXP_LAG = 6
+
+FLOPS = 2 * P * C * 4 * C
+
+
+def transpose_words(nc, bank, first_column, rows_bf16, ident):
+    words = rows_bf16.bitcast(F32)
+    for u in range(2):
+        nc.tensor.transpose(
+            bank[:, first_column + P * u : first_column + P * (u + 1)],
+            words[:, u : 2 * P : 2],
+            ident[:],
+        )
+
+
+def rows_to_columns(nc, psum, small, rows, n_rows, ident, name):
+    flipped = psum.tile([P, BANK], F32, tag="words", name=name + "_flipped")
+    nc.tensor.transpose(flipped[:, 0:P], rows[:].bitcast(F32), ident[:])
+    columns = small.tile([P, n_rows], F32, name=name)
+    nc.vector.tensor_copy(out=columns[:], in_=flipped[:, 0:n_rows])
+    return columns
+
+
+def repeat_on_all_partitions(nc, bank, columns, four_rows, ident):
+    for i, r in enumerate(four_rows):
+        nc.tensor.transpose(
+            bank[:, P * i : P * (i + 1)], columns[:, r : r + 1].to_broadcast([P, P]), ident[:]
+        )
+
+
+def quarter_due(step, lag):
+    piece = step - lag
+    if 0 <= piece < N_PIECES and piece % 2 == 1:
+        return piece // 2
+    return None
+
+
+def tile_probcrossattention_pa_s_kernel(
+    tc, context, eps_noise, Wk, bk, Wv, bv, ln_k_g, ln_k_b, ln_v_g, ln_v_b, out_0, out_1, out_2
+):
+    nc = tc.nc
+    k_mu_out = out_0.flatten_outer_dims()
+    k_var_out = out_1.flatten_outer_dims()
+    v_sample_out = out_2.flatten_outer_dims()
+
+    quarter_weights = (Wv, Wk, Wv, Wk)
+    quarter_first_row = (C, C, 0, 0)
+    quarter_bias_row = (6, 2, 4, 0)
+
+    with ExitStack() as stack:
+        stack.enter_context(tc.manual_schedule())
+        keep = stack.enter_context(tc.tile_pool(name="keep", bufs=1))
+        small = stack.enter_context(tc.tile_pool(name="small", bufs=1))
+        psum = stack.enter_context(tc.psum_pool(name="psum", bufs=4))
+        psum_acc = stack.enter_context(tc.psum_pool(name="psum_acc", bufs=2))
+        psum_affine = stack.enter_context(tc.psum_pool(name="psum_affine", bufs=1))
+
+        ident = keep.tile([P, P], F32)
+        make_identity(nc, ident[:])
+        bias_rows = keep.tile([P, 2 * P], BF16)
+        nc.vector.memset(bias_rows[:], 0.0)
+        affine_rows = keep.tile([P, 2 * P], BF16)
+        nc.vector.memset(affine_rows[:], 0.0)
+        one = small.tile([P, 1], F32)
+        nc.vector.memset(one[:], 1.0)
+        var_eps = small.tile([P, 1], F32)
+        nc.vector.memset(var_eps[:], VAR_EPS)
+        minus_half = small.tile([P, 1], F32)
+        nc.vector.memset(minus_half[:], -0.5)
+
+        ctx_rows = keep.tile([P, C], BF16)
+        nc.sync.dma_start(out=ctx_rows[:], in_=context.flatten_outer_dims())
+        w_rows = [keep.tile([P, 2, C], BF16, name="w_rows%d" % b) for b in range(N_PIECES)]
+        for b in range(N_PIECES):
+            first_row = quarter_first_row[b // 2] + PIECE * (b % 2)
+            nc.sync.dma_start(
+                out=w_rows[b][:],
+                in_=quarter_weights[b // 2][first_row : first_row + PIECE, :].rearrange(
+                    "(p t) k -> p t k", t=2
+                ),
+            )
+            if b == 0:
+                nc.sync.dma_start(out=bias_rows[0:4, :], in_=bk.rearrange("(r c) -> r c", r=4))
+                nc.sync.dma_start(out=bias_rows[4:8, :], in_=bv.rearrange("(r c) -> r c", r=4))
+        for i, vector in enumerate((ln_v_g, ln_v_b, ln_k_g, ln_k_b)):
+            nc.sync.dma_start(
+                out=affine_rows[2 * i : 2 * i + 2, :], in_=vector.rearrange("(r c) -> r c", r=2)
+            )
+        noise = keep.tile([P, C], BF16)
+        nc.sync.dma_start(out=noise[:], in_=eps_noise.flatten_outer_dims())
+
+        ctx_bank = psum.tile([P, BANK], F32, tag="words")
+        transpose_words(nc, ctx_bank, 0, ctx_rows[:], ident)
+        ctx_grouped = keep.tile([P, 4 * P], BF16, align_bytes=64)
+        nc.vector.tensor_copy(
+            out=ctx_grouped[:].bitcast(F32).rearrange("p (n u) -> p n u", u=2),
+            in_=ctx_bank[:, 0 : 2 * P].rearrange("p (u n) -> p n u", u=2),
+        )
+        ctx_codes = keep.tile([P, P], U32, align_bytes=64)
+        ctx_scales = keep.tile([P, P], U8, align_bytes=64)
+        nc.vector.quantize_mx(
+            out=ctx_codes[:].bitcast(FP8X4), scales=ctx_scales[:], in_=ctx_grouped[:]
+        )
+
+        grouped = [
+            keep.tile([P, 4 * PIECE], BF16, align_bytes=64, name="grouped%d" % b)
+            for b in range(N_PIECES)
+        ]
+        w_codes = keep.tile([P, 4, C], U32, align_bytes=64)
+        w_scales = keep.tile([P, 4, C], U8, align_bytes=64)
+        bias_all = keep.tile([P, 4, C], BF16)
+        x_all = keep.tile([P, 4, C], F32)
+        shrunk = keep.tile([P, 2, C], F32)
+        stats = small.tile([P, 2, 6], F32)
+
+        def flip_and_group(b):
+            bank = psum.tile([P, BANK], F32, tag="words", name="w_bank%d" % b)
+            for t in range(2):
+                transpose_words(nc, bank, 2 * P * t, w_rows[b][:, t, :], ident)
+            source = bank[:].rearrange("p (t u n) -> p n t u", t=2, u=2)
+            target = grouped[b][:].bitcast(F32).rearrange("p (n t u) -> p n t u", t=2, u=2)
+            if b % 4 < 3:
+                nc.scalar.copy(out=target, in_=source)
+            else:
+                nc.vector.tensor_copy(out=target, in_=source)
+
+        def quantise(b):
+            cols = slice(PIECE * (b % 2), PIECE * (b % 2 + 1))
+            nc.vector.quantize_mx(
+                out=w_codes[:, b // 2, cols].bitcast(FP8X4),
+                scales=w_scales[:, b // 2, cols],
+                in_=grouped[b][:],
+            )
+
+        def multiply_and_add_bias(quarter):
+            acc = psum_acc.tile([P, C], F32, name="acc")
+            nc.tensor.matmul_mx(
+                out=acc[:],
+                lhsT=ctx_codes[:].bitcast(FP8X4),
+                lhsT_scale=ctx_scales[:],
+                rhs=w_codes[:, quarter, :].bitcast(FP8X4),
+                rhs_scale=w_scales[:, quarter, :],
+                start=True,
+                stop=True,
+            )
+            nc.vector.tensor_tensor(
+                out=x_all[:, quarter, :], in0=acc[:], in1=bias_all[:, quarter, :], op=ALU.add
+            )
+            if quarter >= V_MU:
+                nc.vector.bn_stats(out=stats[:, quarter - V_MU, :], in_=x_all[:, quarter, :])
+
+        def shrink(quarter):
+            nc.scalar.activation(out=shrunk[:, quarter, :], in_=x_all[:, quarter, :], func=ACT.Abs)
+            nc.scalar.activation(
+                out=shrunk[:, quarter, :], in_=shrunk[:, quarter, :], func=ACT.Exp, scale=-1.0
+            )
+
+        def run_steps(first, last):
+            for step in range(first, last):
+                quarter = quarter_due(step, EXP_LAG)
+                if quarter is not None and quarter < V_MU:
+                    shrink(quarter)
+                quarter = quarter_due(step, MULTIPLY_LAG)
+                if quarter is not None:
+                    multiply_and_add_bias(quarter)
+                if 0 <= step - QUANTISE_LAG < N_PIECES:
+                    quantise(step - QUANTISE_LAG)
+                if step < N_PIECES:
+                    flip_and_group(step)
+
+        def spread_biases(first_quarter):
+            four_rows = []
+            for quarter in (first_quarter, first_quarter + 1):
+                four_rows.extend((quarter_bias_row[quarter], quarter_bias_row[quarter] + 1))
+            bank = psum.tile([P, BANK], F32, tag="words", name="bias_bank%d" % first_quarter)
+            repeat_on_all_partitions(nc, bank, bias_columns, four_rows, ident)
+            nc.vector.tensor_copy(
+                out=bias_all[:, first_quarter : first_quarter + 2, :]
+                .rearrange("p q c -> p (q c)")
+                .bitcast(F32),
+                in_=bank[:],
+            )
+
+        def spread_affine(i, name):
+            bank = psum_affine.tile([P, BANK], F32, name=name)
+            repeat_on_all_partitions(nc, bank, affine_columns, range(4 * i, 4 * i + 4), ident)
+            return bank[:].bitcast(BF16)
+
+        def mean_and_rstd(quarter, name):
+            mean_var = small.tile([P, 2], F32, name=name + "_mean_var")
+            nc.vector.bn_aggr(out=mean_var[:], in_=stats[:, quarter - V_MU, :])
+            rstd = small.tile([P, 1], F32, name=name + "_rstd")
+            nc.gpsimd.tensor_scalar(
+                out=rstd[:], in0=mean_var[:, 1:2], scalar1=LN_EPS, scalar2=None, op0=ALU.add
+            )
+            nc.gpsimd.tensor_tensor(out=rstd[:], in0=rstd[:], in1=minus_half[:], op=ALU.pow)
+            return mean_var, rstd
+
+        def centre_and_gain(quarter, mean_var, affine, name):
+            centred = keep.tile([P, C], F32, name=name + "_centred")
+            nc.vector.scalar_tensor_tensor(
+                out=centred[:], in0=x_all[:, quarter, :], scalar=mean_var[:, 0:1],
+                in1=affine[:, 0:C], op0=ALU.subtract, op1=ALU.mult,
+            )
+            return centred
+
+        def scale_and_shift(centred, rstd, affine, name):
+            normed = keep.tile([P, C], F32, name=name + "_mu")
+            nc.vector.scalar_tensor_tensor(
+                out=normed[:], in0=centred[:], scalar=rstd[:, 0:1], in1=affine[:, C : 2 * C],
+                op0=ALU.mult, op1=ALU.add,
+            )
+            return normed
+
+        run_steps(0, 1)
+        bias_columns = rows_to_columns(nc, psum, small, bias_rows, 8, ident, "bias_columns")
+        run_steps(1, 3)
+        spread_biases(V_VAR)
+        spread_biases(V_MU)
+        run_steps(3, N_PIECES + 1)
+        affine_columns = rows_to_columns(nc, psum, small, affine_rows, 8, ident, "affine_columns")
+        run_steps(N_PIECES + 1, K_VAR * 2 + 1 + EXP_LAG + 1)
+
+        log_term = keep.tile([P, 2, C], F32)
+        nc.scalar.activation(out=log_term[:], in_=shrunk[:], func=ACT.Ln, bias=one[:, 0:1])
+        k_var = keep.tile([P, C], F32)
+        nc.gpsimd.tensor_scalar(
+            out=k_var[:], in0=x_all[:, K_VAR, :], scalar1=0.0, scalar2=VAR_EPS,
+            op0=ALU.max, op1=ALU.add,
+        )
+
+        run_steps(K_VAR * 2 + 1 + EXP_LAG + 1, N_PIECES + MULTIPLY_LAG)
+        v_affine = spread_affine(0, "v_affine")
+        k_affine = spread_affine(1, "k_affine")
+
+        v_mean_var, v_rstd = mean_and_rstd(V_MU, "v")
+        k_mean_var, k_rstd = mean_and_rstd(K_MU, "k")
+        v_centred = centre_and_gain(V_MU, v_mean_var, v_affine, "v")
+        v_softplus = keep.tile([P, C], F32)
+        nc.vector.scalar_tensor_tensor(
+            out=v_softplus[:], in0=x_all[:, V_VAR, :], scalar=0.0, in1=log_term[:, V_VAR, :],
+            op0=ALU.max, op1=ALU.add,
+        )
+        k_centred = centre_and_gain(K_MU, k_mean_var, k_affine, "k")
+        v_mu = scale_and_shift(v_centred, v_rstd, v_affine, "v")
+        k_mu = scale_and_shift(k_centred, k_rstd, k_affine, "k")
+        nc.sync.dma_start(out=k_mu_out, in_=k_mu[:])
+        nc.gpsimd.tensor_tensor(out=k_var[:], in0=k_var[:], in1=log_term[:, K_VAR, :], op=ALU.add)
+        nc.sync.dma_start(out=k_var_out, in_=k_var[:])
+
+        v_std = keep.tile([P, C], F32)
+        v_sample = keep.tile([P, C], F32)
+        halves = (slice(0, C // 2), slice(C // 2, C))
+        for cols in halves:
+            nc.scalar.activation(
+                out=v_std[:, cols], in_=v_softplus[:, cols], func=ACT.Sqrt, bias=var_eps[:, 0:1]
+            )
+        for cols in halves:
+            nc.vector.tensor_tensor(
+                out=v_sample[:, cols], in0=v_std[:, cols], in1=noise[:, cols], op=ALU.mult
+            )
+            nc.vector.tensor_tensor(
+                out=v_sample[:, cols], in0=v_sample[:, cols], in1=v_mu[:, cols], op=ALU.add
+            )
+            nc.sync.dma_start(out=v_sample_out[:, cols], in_=v_sample[:, cols])

@@ -1,3 +1,4 @@
+import math
 from contextlib import ExitStack
 
 import concourse.mybir as mybir
@@ -19,6 +20,7 @@ N_PIECES = 4 * C // PIECE
 V_VAR, K_VAR, V_MU, K_MU = 0, 1, 2, 3
 VAR_EPS = 1e-6
 LN_EPS = 1e-5
+TINY = 1e-36
 
 QUANTISE_LAG = 1
 MULTIPLY_LAG = 4
@@ -37,28 +39,6 @@ def transpose_words(nc, bank, first_column, rows_bf16, ident):
         )
 
 
-def rows_to_columns(nc, psum, small, rows, n_rows, ident, name):
-    flipped = psum.tile([P, BANK], F32, tag="words", name=name + "_flipped")
-    nc.tensor.transpose(flipped[:, 0:P], rows[:].bitcast(F32), ident[:])
-    columns = small.tile([P, n_rows], F32, name=name)
-    nc.vector.tensor_copy(out=columns[:], in_=flipped[:, 0:n_rows])
-    return columns
-
-
-def repeat_on_all_partitions(nc, bank, columns, four_rows, ident):
-    for i, r in enumerate(four_rows):
-        nc.tensor.transpose(
-            bank[:, P * i : P * (i + 1)], columns[:, r : r + 1].to_broadcast([P, P]), ident[:]
-        )
-
-
-def quarter_due(step, lag):
-    piece = step - lag
-    if 0 <= piece < N_PIECES and piece % 2 == 1:
-        return piece // 2
-    return None
-
-
 def tile_probcrossattention_pa_s_kernel(
     tc, context, eps_noise, Wk, bk, Wv, bv, ln_k_g, ln_k_b, ln_v_g, ln_v_b, out_0, out_1, out_2
 ):
@@ -69,33 +49,26 @@ def tile_probcrossattention_pa_s_kernel(
 
     quarter_weights = (Wv, Wk, Wv, Wk)
     quarter_first_row = (C, C, 0, 0)
-    quarter_bias_row = (6, 2, 4, 0)
 
     with ExitStack() as stack:
         stack.enter_context(tc.manual_schedule())
         keep = stack.enter_context(tc.tile_pool(name="keep", bufs=1))
         small = stack.enter_context(tc.tile_pool(name="small", bufs=1))
-        psum = stack.enter_context(tc.psum_pool(name="psum", bufs=4))
+        psum = stack.enter_context(tc.psum_pool(name="psum", bufs=6))
         psum_acc = stack.enter_context(tc.psum_pool(name="psum_acc", bufs=2))
-        psum_affine = stack.enter_context(tc.psum_pool(name="psum_affine", bufs=1))
 
         ident = keep.tile([P, P], F32)
         make_identity(nc, ident[:])
-        bias_rows = keep.tile([P, 2 * P], BF16)
-        nc.vector.memset(bias_rows[:], 0.0)
-        affine_rows = keep.tile([P, 2 * P], BF16)
-        nc.vector.memset(affine_rows[:], 0.0)
-        one = small.tile([P, 1], F32)
-        nc.vector.memset(one[:], 1.0)
-        var_eps = small.tile([P, 1], F32)
-        nc.vector.memset(var_eps[:], VAR_EPS)
         minus_half = small.tile([P, 1], F32)
         nc.vector.memset(minus_half[:], -0.5)
+        warm = small.tile([P, 1], F32)
+        nc.scalar.activation(out=warm[:], in_=minus_half[:], func=ACT.Sigmoid)
 
         ctx_rows = keep.tile([P, C], BF16)
         nc.sync.dma_start(out=ctx_rows[:], in_=context.flatten_outer_dims())
         w_rows = [keep.tile([P, 2, C], BF16, name="w_rows%d" % b) for b in range(N_PIECES)]
-        for b in range(N_PIECES):
+
+        def load_piece(b):
             first_row = quarter_first_row[b // 2] + PIECE * (b % 2)
             nc.sync.dma_start(
                 out=w_rows[b][:],
@@ -103,47 +76,56 @@ def tile_probcrossattention_pa_s_kernel(
                     "(p t) k -> p t k", t=2
                 ),
             )
-            if b == 0:
-                nc.sync.dma_start(out=bias_rows[0:4, :], in_=bk.rearrange("(r c) -> r c", r=4))
-                nc.sync.dma_start(out=bias_rows[4:8, :], in_=bv.rearrange("(r c) -> r c", r=4))
-        for i, vector in enumerate((ln_v_g, ln_v_b, ln_k_g, ln_k_b)):
-            nc.sync.dma_start(
-                out=affine_rows[2 * i : 2 * i + 2, :], in_=vector.rearrange("(r c) -> r c", r=2)
-            )
+
+        def spread(vector, name):
+            tile = keep.tile([P, C], BF16, name=name)
+            nc.sync.dma_start(out=tile[:], in_=vector.partition_broadcast(P))
+            return tile
+
+        quarter_bias = {}
+        load_piece(0)
+        load_piece(1)
+        quarter_bias[V_VAR] = spread(bv[C : 2 * C], "bias_v_var")
+        load_piece(2)
+        load_piece(3)
+        quarter_bias[K_VAR] = spread(bk[C : 2 * C], "bias_k_var")
+        for b in range(4, N_PIECES):
+            load_piece(b)
+        quarter_bias[V_MU] = spread(bv[0:C], "bias_v_mu")
+        quarter_bias[K_MU] = spread(bk[0:C], "bias_k_mu")
+        v_g = spread(ln_v_g, "v_g")
+        k_g = spread(ln_k_g, "k_g")
+        k_b = spread(ln_k_b, "k_b")
+        v_b = spread(ln_v_b, "v_b")
         noise = keep.tile([P, C], BF16)
         nc.sync.dma_start(out=noise[:], in_=eps_noise.flatten_outer_dims())
 
-        ctx_bank = psum.tile([P, BANK], F32, tag="words")
-        transpose_words(nc, ctx_bank, 0, ctx_rows[:], ident)
         ctx_grouped = keep.tile([P, 4 * P], BF16, align_bytes=64)
-        nc.vector.tensor_copy(
-            out=ctx_grouped[:].bitcast(F32).rearrange("p (n u) -> p n u", u=2),
-            in_=ctx_bank[:, 0 : 2 * P].rearrange("p (u n) -> p n u", u=2),
-        )
         ctx_codes = keep.tile([P, P], U32, align_bytes=64)
         ctx_scales = keep.tile([P, P], U8, align_bytes=64)
-        nc.vector.quantize_mx(
-            out=ctx_codes[:].bitcast(FP8X4), scales=ctx_scales[:], in_=ctx_grouped[:]
-        )
-
         grouped = [
             keep.tile([P, 4 * PIECE], BF16, align_bytes=64, name="grouped%d" % b)
             for b in range(N_PIECES)
         ]
         w_codes = keep.tile([P, 4, C], U32, align_bytes=64)
         w_scales = keep.tile([P, 4, C], U8, align_bytes=64)
-        bias_all = keep.tile([P, 4, C], BF16)
         x_all = keep.tile([P, 4, C], F32)
-        shrunk = keep.tile([P, 2, C], F32)
+        sig = keep.tile([P, 2, C], F32)
+        log_term = keep.tile([P, 2, C], F32)
         stats = small.tile([P, 2, 6], F32)
+        banks = {}
+        accs = {}
 
-        def flip_and_group(b):
+        def flip(b):
             bank = psum.tile([P, BANK], F32, tag="words", name="w_bank%d" % b)
             for t in range(2):
                 transpose_words(nc, bank, 2 * P * t, w_rows[b][:, t, :], ident)
-            source = bank[:].rearrange("p (t u n) -> p n t u", t=2, u=2)
+            banks[b] = bank
+
+        def group(b, engine):
+            source = banks[b][:].rearrange("p (t u n) -> p n t u", t=2, u=2)
             target = grouped[b][:].bitcast(F32).rearrange("p (n t u) -> p n t u", t=2, u=2)
-            if b % 4 < 3:
+            if engine == "scalar":
                 nc.scalar.copy(out=target, in_=source)
             else:
                 nc.vector.tensor_copy(out=target, in_=source)
@@ -156,7 +138,7 @@ def tile_probcrossattention_pa_s_kernel(
                 in_=grouped[b][:],
             )
 
-        def multiply_and_add_bias(quarter):
+        def multiply(quarter):
             acc = psum_acc.tile([P, C], F32, name="acc")
             nc.tensor.matmul_mx(
                 out=acc[:],
@@ -167,48 +149,34 @@ def tile_probcrossattention_pa_s_kernel(
                 start=True,
                 stop=True,
             )
+            accs[quarter] = acc
+
+        def add_bias(quarter):
             nc.vector.tensor_tensor(
-                out=x_all[:, quarter, :], in0=acc[:], in1=bias_all[:, quarter, :], op=ALU.add
+                out=x_all[:, quarter, :], in0=accs[quarter][:], in1=quarter_bias[quarter][:], op=ALU.add
             )
-            if quarter >= V_MU:
-                nc.vector.bn_stats(out=stats[:, quarter - V_MU, :], in_=x_all[:, quarter, :])
 
-        def shrink(quarter):
-            nc.scalar.activation(out=shrunk[:, quarter, :], in_=x_all[:, quarter, :], func=ACT.Abs)
+        def statistics(quarter):
+            nc.vector.bn_stats(out=stats[:, quarter - V_MU, :], in_=x_all[:, quarter, :])
+
+        def sigmoid(quarter):
             nc.scalar.activation(
-                out=shrunk[:, quarter, :], in_=shrunk[:, quarter, :], func=ACT.Exp, scale=-1.0
+                out=sig[:, quarter, :], in_=x_all[:, quarter, :], func=ACT.Sigmoid, scale=-1.0
             )
 
-        def run_steps(first, last):
-            for step in range(first, last):
-                quarter = quarter_due(step, EXP_LAG)
-                if quarter is not None and quarter < V_MU:
-                    shrink(quarter)
-                quarter = quarter_due(step, MULTIPLY_LAG)
-                if quarter is not None:
-                    multiply_and_add_bias(quarter)
-                if 0 <= step - QUANTISE_LAG < N_PIECES:
-                    quantise(step - QUANTISE_LAG)
-                if step < N_PIECES:
-                    flip_and_group(step)
-
-        def spread_biases(first_quarter):
-            four_rows = []
-            for quarter in (first_quarter, first_quarter + 1):
-                four_rows.extend((quarter_bias_row[quarter], quarter_bias_row[quarter] + 1))
-            bank = psum.tile([P, BANK], F32, tag="words", name="bias_bank%d" % first_quarter)
-            repeat_on_all_partitions(nc, bank, bias_columns, four_rows, ident)
-            nc.vector.tensor_copy(
-                out=bias_all[:, first_quarter : first_quarter + 2, :]
-                .rearrange("p q c -> p (q c)")
-                .bitcast(F32),
-                in_=bank[:],
+        def logarithm(quarter, scale):
+            nc.scalar.activation(
+                out=log_term[:, quarter, :], in_=sig[:, quarter, :], func=ACT.Ln, bias=TINY,
+                scale=scale,
             )
 
-        def spread_affine(i, name):
-            bank = psum_affine.tile([P, BANK], F32, name=name)
-            repeat_on_all_partitions(nc, bank, affine_columns, range(4 * i, 4 * i + 4), ident)
-            return bank[:].bitcast(BF16)
+        def softplus(quarter, name):
+            result = keep.tile([P, C], F32, name=name)
+            nc.vector.scalar_tensor_tensor(
+                out=result[:], in0=log_term[:, quarter, :], scalar=-1.0, in1=x_all[:, quarter, :],
+                op0=ALU.mult, op1=ALU.max,
+            )
+            return result
 
         def mean_and_rstd(quarter, name):
             mean_var = small.tile([P, 2], F32, name=name + "_mean_var")
@@ -220,70 +188,90 @@ def tile_probcrossattention_pa_s_kernel(
             nc.gpsimd.tensor_tensor(out=rstd[:], in0=rstd[:], in1=minus_half[:], op=ALU.pow)
             return mean_var, rstd
 
-        def centre_and_gain(quarter, mean_var, affine, name):
+        def centre_and_gain(quarter, mean_var, gain, name):
             centred = keep.tile([P, C], F32, name=name + "_centred")
             nc.vector.scalar_tensor_tensor(
                 out=centred[:], in0=x_all[:, quarter, :], scalar=mean_var[:, 0:1],
-                in1=affine[:, 0:C], op0=ALU.subtract, op1=ALU.mult,
+                in1=gain[:], op0=ALU.subtract, op1=ALU.mult,
             )
             return centred
 
-        def scale_and_shift(centred, rstd, affine, name):
+        def scale_and_shift(centred, rstd, shift, name):
             normed = keep.tile([P, C], F32, name=name + "_mu")
             nc.vector.scalar_tensor_tensor(
-                out=normed[:], in0=centred[:], scalar=rstd[:, 0:1], in1=affine[:, C : 2 * C],
+                out=normed[:], in0=centred[:], scalar=rstd[:, 0:1], in1=shift[:],
                 op0=ALU.mult, op1=ALU.add,
             )
             return normed
 
-        run_steps(0, 1)
-        bias_columns = rows_to_columns(nc, psum, small, bias_rows, 8, ident, "bias_columns")
-        run_steps(1, 3)
-        spread_biases(V_VAR)
-        spread_biases(V_MU)
-        run_steps(3, N_PIECES + 1)
-        affine_columns = rows_to_columns(nc, psum, small, affine_rows, 8, ident, "affine_columns")
-        run_steps(N_PIECES + 1, K_VAR * 2 + 1 + EXP_LAG + 1)
-
-        log_term = keep.tile([P, 2, C], F32)
-        nc.scalar.activation(out=log_term[:], in_=shrunk[:], func=ACT.Ln, bias=one[:, 0:1])
-        k_var = keep.tile([P, C], F32)
-        nc.gpsimd.tensor_scalar(
-            out=k_var[:], in0=x_all[:, K_VAR, :], scalar1=0.0, scalar2=VAR_EPS,
-            op0=ALU.max, op1=ALU.add,
+        ctx_bank = psum.tile([P, BANK], F32, tag="words")
+        transpose_words(nc, ctx_bank, 0, ctx_rows[:], ident)
+        nc.vector.tensor_copy(
+            out=ctx_grouped[:].bitcast(F32).rearrange("p (n u) -> p n u", u=2),
+            in_=ctx_bank[:, 0 : 2 * P].rearrange("p (u n) -> p n u", u=2),
         )
-
-        run_steps(K_VAR * 2 + 1 + EXP_LAG + 1, N_PIECES + MULTIPLY_LAG)
-        v_affine = spread_affine(0, "v_affine")
-        k_affine = spread_affine(1, "k_affine")
-
+        nc.vector.quantize_mx(
+            out=ctx_codes[:].bitcast(FP8X4), scales=ctx_scales[:], in_=ctx_grouped[:]
+        )
+        flip(0)
+        group(0, "scalar")
+        flip(1)
+        group(1, "scalar")
+        quantise(0)
+        flip(2)
+        group(2, "scalar")
+        quantise(1)
+        flip(3)
+        group(3, "scalar")
+        quantise(2)
+        multiply(V_VAR)
+        add_bias(V_VAR)
+        flip(4)
+        group(4, "scalar")
+        quantise(3)
+        flip(5)
+        group(5, "scalar")
+        sigmoid(V_VAR)
+        quantise(4)
+        flip(6)
+        group(6, "scalar")
+        multiply(K_VAR)
+        add_bias(K_VAR)
+        quantise(5)
+        sigmoid(K_VAR)
+        flip(7)
+        group(7, "scalar")
+        multiply(V_MU)
+        quantise(6)
+        add_bias(V_MU)
+        quantise(7)
+        multiply(K_MU)
+        statistics(V_MU)
         v_mean_var, v_rstd = mean_and_rstd(V_MU, "v")
+        add_bias(K_MU)
+        statistics(K_MU)
         k_mean_var, k_rstd = mean_and_rstd(K_MU, "k")
-        v_centred = centre_and_gain(V_MU, v_mean_var, v_affine, "v")
-        v_softplus = keep.tile([P, C], F32)
-        nc.vector.scalar_tensor_tensor(
-            out=v_softplus[:], in0=x_all[:, V_VAR, :], scalar=0.0, in1=log_term[:, V_VAR, :],
-            op0=ALU.max, op1=ALU.add,
-        )
-        k_centred = centre_and_gain(K_MU, k_mean_var, k_affine, "k")
-        v_mu = scale_and_shift(v_centred, v_rstd, v_affine, "v")
-        k_mu = scale_and_shift(k_centred, k_rstd, k_affine, "k")
-        nc.sync.dma_start(out=k_mu_out, in_=k_mu[:])
-        nc.gpsimd.tensor_tensor(out=k_var[:], in0=k_var[:], in1=log_term[:, K_VAR, :], op=ALU.add)
+        logarithm(V_VAR, math.exp(-VAR_EPS))
+        logarithm(K_VAR, math.exp(-VAR_EPS))
+        v_var = softplus(V_VAR, "v_var")
+        v_centred = centre_and_gain(V_MU, v_mean_var, v_g, "v")
+        k_centred = centre_and_gain(K_MU, k_mean_var, k_g, "k")
+        k_var = softplus(K_VAR, "k_var")
         nc.sync.dma_start(out=k_var_out, in_=k_var[:])
-
+        k_mu = scale_and_shift(k_centred, k_rstd, k_b, "k")
+        nc.sync.dma_start(out=k_mu_out, in_=k_mu[:])
+        v_mu = scale_and_shift(v_centred, v_rstd, v_b, "v")
         v_std = keep.tile([P, C], F32)
+        spread_noise = keep.tile([P, C], F32)
         v_sample = keep.tile([P, C], F32)
         halves = (slice(0, C // 2), slice(C // 2, C))
         for cols in halves:
-            nc.scalar.activation(
-                out=v_std[:, cols], in_=v_softplus[:, cols], func=ACT.Sqrt, bias=var_eps[:, 0:1]
+            nc.scalar.activation(out=v_std[:, cols], in_=v_var[:, cols], func=ACT.Sqrt)
+            nc.gpsimd.tensor_tensor(
+                out=spread_noise[:, cols], in0=v_std[:, cols], in1=noise[:, cols], op=ALU.mult
             )
         for cols in halves:
             nc.vector.tensor_tensor(
-                out=v_sample[:, cols], in0=v_std[:, cols], in1=noise[:, cols], op=ALU.mult
-            )
-            nc.vector.tensor_tensor(
-                out=v_sample[:, cols], in0=v_sample[:, cols], in1=v_mu[:, cols], op=ALU.add
+                out=v_sample[:, cols], in0=spread_noise[:, cols], in1=v_mu[:, cols], op=ALU.add
             )
             nc.sync.dma_start(out=v_sample_out[:, cols], in_=v_sample[:, cols])

@@ -15,16 +15,14 @@ ACT = mybir.ActivationFunctionType
 P = 128
 C = 512
 BANK = 512
-PIECE = 256
-N_PIECES = 4 * C // PIECE
 V_VAR, K_VAR, V_MU, K_MU = 0, 1, 2, 3
+PIECES = ((V_VAR, 0, 128), (V_VAR, 128, 128), (V_VAR, 256, 256)) + tuple(
+    (quarter, first, 256) for quarter in (K_VAR, V_MU, K_MU) for first in (0, 256)
+)
 VAR_EPS = 1e-6
 LN_EPS = 1e-5
 TINY = 1e-36
-
-QUANTISE_LAG = 1
-MULTIPLY_LAG = 4
-EXP_LAG = 6
+WARM_UPS = 3
 
 FLOPS = 2 * P * C * 4 * C
 
@@ -39,6 +37,21 @@ def transpose_words(nc, bank, first_column, rows_bf16, ident):
         )
 
 
+def rows_to_columns(nc, psum, small, rows, n_rows, ident, name):
+    flipped = psum.tile([P, BANK], F32, tag="words", name=name + "_flipped")
+    nc.tensor.transpose(flipped[:, 0:P], rows[:].bitcast(F32), ident[:])
+    columns = small.tile([P, n_rows], F32, name=name)
+    nc.vector.tensor_copy(out=columns[:], in_=flipped[:, 0:n_rows])
+    return columns
+
+
+def repeat_on_all_partitions(nc, bank, columns, four_rows, ident):
+    for i, r in enumerate(four_rows):
+        nc.tensor.transpose(
+            bank[:, P * i : P * (i + 1)], columns[:, r : r + 1].to_broadcast([P, P]), ident[:]
+        )
+
+
 def tile_probcrossattention_pa_s_kernel(
     tc, context, eps_noise, Wk, bk, Wv, bv, ln_k_g, ln_k_b, ln_v_g, ln_v_b, out_0, out_1, out_2
 ):
@@ -49,54 +62,62 @@ def tile_probcrossattention_pa_s_kernel(
 
     quarter_weights = (Wv, Wk, Wv, Wk)
     quarter_first_row = (C, C, 0, 0)
+    quarter_bias_row = (6, 2, 4, 0)
 
     with ExitStack() as stack:
         stack.enter_context(tc.manual_schedule())
         keep = stack.enter_context(tc.tile_pool(name="keep", bufs=1))
         small = stack.enter_context(tc.tile_pool(name="small", bufs=1))
-        psum = stack.enter_context(tc.psum_pool(name="psum", bufs=6))
+        psum = stack.enter_context(tc.psum_pool(name="psum", bufs=4))
         psum_acc = stack.enter_context(tc.psum_pool(name="psum_acc", bufs=2))
+        psum_affine = stack.enter_context(tc.psum_pool(name="psum_affine", bufs=1))
 
+        zeros = keep.tile([P, P], F32)
+        nc.vector.memset(zeros[:], 0.0)
         ident = keep.tile([P, P], F32)
         make_identity(nc, ident[:])
         minus_half = small.tile([P, 1], F32)
         nc.vector.memset(minus_half[:], -0.5)
+        bias_rows = keep.tile([P, 2 * P], BF16)
+        nc.vector.memset(bias_rows[:], 0.0)
+        affine_rows = keep.tile([P, 2 * P], BF16)
+        nc.vector.memset(affine_rows[:], 0.0)
         warm = small.tile([P, 1], F32)
         nc.scalar.activation(out=warm[:], in_=minus_half[:], func=ACT.Sigmoid)
 
+        warm_bank = psum.tile([P, BANK], F32, tag="words", name="warm_bank")
+        for i in range(WARM_UPS):
+            nc.tensor.matmul(warm_bank[:, 0:P], zeros[:], zeros[:], start=True, stop=True)
+
         ctx_rows = keep.tile([P, C], BF16)
-        nc.sync.dma_start(out=ctx_rows[:], in_=context.flatten_outer_dims())
-        w_rows = [keep.tile([P, 2, C], BF16, name="w_rows%d" % b) for b in range(N_PIECES)]
+        w_rows = [
+            keep.tile([P, rows // P, C], BF16, name="w_rows%d" % b)
+            for b, (quarter, first, rows) in enumerate(PIECES)
+        ]
 
         def load_piece(b):
-            first_row = quarter_first_row[b // 2] + PIECE * (b % 2)
+            quarter, first, rows = PIECES[b]
+            first_row = quarter_first_row[quarter] + first
             nc.sync.dma_start(
                 out=w_rows[b][:],
-                in_=quarter_weights[b // 2][first_row : first_row + PIECE, :].rearrange(
-                    "(p t) k -> p t k", t=2
+                in_=quarter_weights[quarter][first_row : first_row + rows, :].rearrange(
+                    "(p t) k -> p t k", p=P
                 ),
             )
 
-        def spread(vector, name):
-            tile = keep.tile([P, C], BF16, name=name)
-            nc.sync.dma_start(out=tile[:], in_=vector.partition_broadcast(P))
-            return tile
-
-        quarter_bias = {}
         load_piece(0)
+        nc.sync.dma_start(out=bias_rows[0:4, :], in_=bk.rearrange("(r c) -> r c", r=4))
+        nc.sync.dma_start(out=bias_rows[4:8, :], in_=bv.rearrange("(r c) -> r c", r=4))
         load_piece(1)
-        quarter_bias[V_VAR] = spread(bv[C : 2 * C], "bias_v_var")
-        load_piece(2)
-        load_piece(3)
-        quarter_bias[K_VAR] = spread(bk[C : 2 * C], "bias_k_var")
-        for b in range(4, N_PIECES):
+        nc.sync.dma_start(out=ctx_rows[:], in_=context.flatten_outer_dims())
+        for b in range(2, 6):
             load_piece(b)
-        quarter_bias[V_MU] = spread(bv[0:C], "bias_v_mu")
-        quarter_bias[K_MU] = spread(bk[0:C], "bias_k_mu")
-        v_g = spread(ln_v_g, "v_g")
-        k_g = spread(ln_k_g, "k_g")
-        k_b = spread(ln_k_b, "k_b")
-        v_b = spread(ln_v_b, "v_b")
+        for i, vector in enumerate((ln_v_g, ln_v_b, ln_k_g, ln_k_b)):
+            nc.sync.dma_start(
+                out=affine_rows[2 * i : 2 * i + 2, :], in_=vector.rearrange("(r c) -> r c", r=2)
+            )
+        for b in range(6, len(PIECES)):
+            load_piece(b)
         noise = keep.tile([P, C], BF16)
         nc.sync.dma_start(out=noise[:], in_=eps_noise.flatten_outer_dims())
 
@@ -104,37 +125,40 @@ def tile_probcrossattention_pa_s_kernel(
         ctx_codes = keep.tile([P, P], U32, align_bytes=64)
         ctx_scales = keep.tile([P, P], U8, align_bytes=64)
         grouped = [
-            keep.tile([P, 4 * PIECE], BF16, align_bytes=64, name="grouped%d" % b)
-            for b in range(N_PIECES)
+            keep.tile([P, 4 * rows], BF16, align_bytes=64, name="grouped%d" % b)
+            for b, (quarter, first, rows) in enumerate(PIECES)
         ]
         w_codes = keep.tile([P, 4, C], U32, align_bytes=64)
         w_scales = keep.tile([P, 4, C], U8, align_bytes=64)
         x_all = keep.tile([P, 4, C], F32)
         sig = keep.tile([P, 2, C], F32)
         log_term = keep.tile([P, 2, C], F32)
+        bias_all = keep.tile([P, 4, C], BF16)
         stats = small.tile([P, 2, 6], F32)
         banks = {}
         accs = {}
 
         def flip(b):
             bank = psum.tile([P, BANK], F32, tag="words", name="w_bank%d" % b)
-            for t in range(2):
+            for t in range(PIECES[b][2] // P):
                 transpose_words(nc, bank, 2 * P * t, w_rows[b][:, t, :], ident)
             banks[b] = bank
 
         def group(b, engine):
-            source = banks[b][:].rearrange("p (t u n) -> p n t u", t=2, u=2)
-            target = grouped[b][:].bitcast(F32).rearrange("p (n t u) -> p n t u", t=2, u=2)
+            rows = PIECES[b][2]
+            source = banks[b][:, 0 : 2 * rows].rearrange("p (t u n) -> p n t u", u=2, n=P)
+            target = grouped[b][:].bitcast(F32).rearrange("p (n t u) -> p n t u", u=2, n=P)
             if engine == "scalar":
                 nc.scalar.copy(out=target, in_=source)
             else:
                 nc.vector.tensor_copy(out=target, in_=source)
 
         def quantise(b):
-            cols = slice(PIECE * (b % 2), PIECE * (b % 2 + 1))
+            quarter, first, rows = PIECES[b]
+            cols = slice(first, first + rows)
             nc.vector.quantize_mx(
-                out=w_codes[:, b // 2, cols].bitcast(FP8X4),
-                scales=w_scales[:, b // 2, cols],
+                out=w_codes[:, quarter, cols].bitcast(FP8X4),
+                scales=w_scales[:, quarter, cols],
                 in_=grouped[b][:],
             )
 
@@ -153,8 +177,26 @@ def tile_probcrossattention_pa_s_kernel(
 
         def add_bias(quarter):
             nc.vector.tensor_tensor(
-                out=x_all[:, quarter, :], in0=accs[quarter][:], in1=quarter_bias[quarter][:], op=ALU.add
+                out=x_all[:, quarter, :], in0=accs[quarter][:], in1=bias_all[:, quarter, :], op=ALU.add
             )
+
+        def spread_biases(first_quarter, copy):
+            four_rows = []
+            for quarter in (first_quarter, first_quarter + 1):
+                four_rows.extend((quarter_bias_row[quarter], quarter_bias_row[quarter] + 1))
+            bank = psum.tile([P, BANK], F32, tag="words", name="bias_bank%d" % first_quarter)
+            repeat_on_all_partitions(nc, bank, bias_columns, four_rows, ident)
+            copy(
+                out=bias_all[:, first_quarter : first_quarter + 2, :]
+                .rearrange("p q c -> p (q c)")
+                .bitcast(F32),
+                in_=bank[:],
+            )
+
+        def spread_affine(i, name):
+            bank = psum_affine.tile([P, BANK], F32, name=name)
+            repeat_on_all_partitions(nc, bank, affine_columns, range(4 * i, 4 * i + 4), ident)
+            return bank[:].bitcast(BF16)
 
         def statistics(quarter):
             nc.vector.bn_stats(out=stats[:, quarter - V_MU, :], in_=x_all[:, quarter, :])
@@ -192,82 +234,102 @@ def tile_probcrossattention_pa_s_kernel(
             centred = keep.tile([P, C], F32, name=name + "_centred")
             nc.vector.scalar_tensor_tensor(
                 out=centred[:], in0=x_all[:, quarter, :], scalar=mean_var[:, 0:1],
-                in1=gain[:], op0=ALU.subtract, op1=ALU.mult,
+                in1=gain, op0=ALU.subtract, op1=ALU.mult,
             )
             return centred
 
         def scale_and_shift(centred, rstd, shift, name):
             normed = keep.tile([P, C], F32, name=name + "_mu")
             nc.vector.scalar_tensor_tensor(
-                out=normed[:], in0=centred[:], scalar=rstd[:, 0:1], in1=shift[:],
+                out=normed[:], in0=centred[:], scalar=rstd[:, 0:1], in1=shift,
                 op0=ALU.mult, op1=ALU.add,
             )
             return normed
 
-        ctx_bank = psum.tile([P, BANK], F32, tag="words")
-        transpose_words(nc, ctx_bank, 0, ctx_rows[:], ident)
-        nc.vector.tensor_copy(
-            out=ctx_grouped[:].bitcast(F32).rearrange("p (n u) -> p n u", u=2),
-            in_=ctx_bank[:, 0 : 2 * P].rearrange("p (u n) -> p n u", u=2),
-        )
-        nc.vector.quantize_mx(
-            out=ctx_codes[:].bitcast(FP8X4), scales=ctx_scales[:], in_=ctx_grouped[:]
-        )
+        def flip_context():
+            bank = psum.tile([P, BANK], F32, tag="words", name="ctx_bank")
+            transpose_words(nc, bank, 0, ctx_rows[:], ident)
+            return bank
+
+        def group_context(bank):
+            nc.vector.tensor_copy(
+                out=ctx_grouped[:].bitcast(F32).rearrange("p (n u) -> p n u", u=2),
+                in_=bank[:, 0 : 2 * P].rearrange("p (u n) -> p n u", u=2),
+            )
+
+        def quantise_context():
+            nc.vector.quantize_mx(
+                out=ctx_codes[:].bitcast(FP8X4), scales=ctx_scales[:], in_=ctx_grouped[:]
+            )
+
         flip(0)
         group(0, "scalar")
+        bias_columns = rows_to_columns(nc, psum, small, bias_rows, 8, ident, "bias_columns")
         flip(1)
         group(1, "scalar")
         quantise(0)
+        spread_biases(V_VAR, nc.scalar.copy)
+        ctx_bank = flip_context()
+        group_context(ctx_bank)
+        quantise(1)
         flip(2)
         group(2, "scalar")
-        quantise(1)
+        quantise_context()
         flip(3)
         group(3, "scalar")
         quantise(2)
-        multiply(V_VAR)
-        add_bias(V_VAR)
         flip(4)
         group(4, "scalar")
-        quantise(3)
         flip(5)
         group(5, "scalar")
-        sigmoid(V_VAR)
-        quantise(4)
+        quantise(3)
+        affine_columns = rows_to_columns(nc, psum, small, affine_rows, 8, ident, "affine_columns")
+        multiply(V_VAR)
+        add_bias(V_VAR)
         flip(6)
         group(6, "scalar")
-        multiply(K_VAR)
-        add_bias(K_VAR)
-        quantise(5)
-        sigmoid(K_VAR)
+        quantise(4)
         flip(7)
         group(7, "scalar")
-        multiply(V_MU)
+        quantise(5)
+        spread_biases(V_MU, nc.scalar.copy)
+        multiply(K_VAR)
         quantise(6)
-        add_bias(V_MU)
+        add_bias(K_VAR)
+        flip(8)
+        group(8, "scalar")
+        multiply(V_MU)
         quantise(7)
+        v_affine = spread_affine(0, "v_affine")
+        sigmoid(V_VAR)
+        sigmoid(K_VAR)
+        add_bias(V_MU)
+        quantise(8)
         multiply(K_MU)
+        k_affine = spread_affine(1, "k_affine")
         statistics(V_MU)
         v_mean_var, v_rstd = mean_and_rstd(V_MU, "v")
         add_bias(K_MU)
+        v_centred = centre_and_gain(V_MU, v_mean_var, v_affine[:, 0:C], "v")
         statistics(K_MU)
         k_mean_var, k_rstd = mean_and_rstd(K_MU, "k")
+        k_centred = centre_and_gain(K_MU, k_mean_var, k_affine[:, 0:C], "k")
+
         logarithm(V_VAR, math.exp(-VAR_EPS))
         logarithm(K_VAR, math.exp(-VAR_EPS))
         v_var = softplus(V_VAR, "v_var")
-        v_centred = centre_and_gain(V_MU, v_mean_var, v_g, "v")
-        k_centred = centre_and_gain(K_MU, k_mean_var, k_g, "k")
         k_var = softplus(K_VAR, "k_var")
         nc.sync.dma_start(out=k_var_out, in_=k_var[:])
-        k_mu = scale_and_shift(k_centred, k_rstd, k_b, "k")
+        k_mu = scale_and_shift(k_centred, k_rstd, k_affine[:, C : 2 * C], "k")
         nc.sync.dma_start(out=k_mu_out, in_=k_mu[:])
-        v_mu = scale_and_shift(v_centred, v_rstd, v_b, "v")
+        v_mu = scale_and_shift(v_centred, v_rstd, v_affine[:, C : 2 * C], "v")
         v_std = keep.tile([P, C], F32)
         spread_noise = keep.tile([P, C], F32)
         v_sample = keep.tile([P, C], F32)
         halves = (slice(0, C // 2), slice(C // 2, C))
         for cols in halves:
             nc.scalar.activation(out=v_std[:, cols], in_=v_var[:, cols], func=ACT.Sqrt)
-            nc.gpsimd.tensor_tensor(
+            nc.vector.tensor_tensor(
                 out=spread_noise[:, cols], in0=v_std[:, cols], in1=noise[:, cols], op=ALU.mult
             )
         for cols in halves:

@@ -308,21 +308,20 @@ def tile_probcrossattention_pa_s_kernel(
         multiply(K_MU)
         k_affine = spread_affine(1, "k_affine")
         statistics(V_MU)
-        v_mean_var, v_rstd = mean_and_rstd(V_MU, "v")
         add_bias(K_MU)
-        v_centred = centre_and_gain(V_MU, v_mean_var, v_affine[:, 0:C], "v")
+        v_mean_var, v_rstd = mean_and_rstd(V_MU, "v")
         statistics(K_MU)
+        v_centred = centre_and_gain(V_MU, v_mean_var, v_affine[:, 0:C], "v")
         k_mean_var, k_rstd = mean_and_rstd(K_MU, "k")
+        v_mu = scale_and_shift(v_centred, v_rstd, v_affine[:, C : 2 * C], "v")
         k_centred = centre_and_gain(K_MU, k_mean_var, k_affine[:, 0:C], "k")
-
         logarithm(V_VAR, math.exp(-VAR_EPS))
         logarithm(K_VAR, math.exp(-VAR_EPS))
         v_var = softplus(V_VAR, "v_var")
-        k_var = softplus(K_VAR, "k_var")
-        nc.sync.dma_start(out=k_var_out, in_=k_var[:])
         k_mu = scale_and_shift(k_centred, k_rstd, k_affine[:, C : 2 * C], "k")
         nc.sync.dma_start(out=k_mu_out, in_=k_mu[:])
-        v_mu = scale_and_shift(v_centred, v_rstd, v_affine[:, C : 2 * C], "v")
+        k_var = softplus(K_VAR, "k_var")
+        nc.sync.dma_start(out=k_var_out, in_=k_var[:])
         v_std = keep.tile([P, C], F32)
         spread_noise = keep.tile([P, C], F32)
         v_sample = keep.tile([P, C], F32)

@@ -72,22 +72,21 @@ def tile_probcrossattention_pa_s_kernel(
         psum_acc = stack.enter_context(tc.psum_pool(name="psum_acc", bufs=2))
         psum_affine = stack.enter_context(tc.psum_pool(name="psum_affine", bufs=1))
 
-        zeros = keep.tile([P, P], F32)
-        nc.vector.memset(zeros[:], 0.0)
+        bias_rows = keep.tile([P, 2 * P], BF16)
+        nc.vector.memset(bias_rows[:].bitcast(F32), 0.0)
+        affine_rows = keep.tile([P, 2 * P], BF16)
+        nc.vector.memset(affine_rows[:].bitcast(F32), 0.0)
         ident = keep.tile([P, P], F32)
         make_identity(nc, ident[:])
-        minus_half = small.tile([P, 1], F32)
+        minus_half = small.tile([P, 2], F32)
         nc.vector.memset(minus_half[:], -0.5)
-        bias_rows = keep.tile([P, 2 * P], BF16)
-        nc.vector.memset(bias_rows[:], 0.0)
-        affine_rows = keep.tile([P, 2 * P], BF16)
-        nc.vector.memset(affine_rows[:], 0.0)
         warm = small.tile([P, 1], F32)
-        nc.scalar.activation(out=warm[:], in_=minus_half[:], func=ACT.Sigmoid)
+        nc.scalar.activation(out=warm[:], in_=minus_half[:, 0:1], func=ACT.Sigmoid)
 
+        zeros = affine_rows[:].bitcast(F32)
         warm_bank = psum.tile([P, BANK], F32, tag="words", name="warm_bank")
         for i in range(WARM_UPS):
-            nc.tensor.matmul(warm_bank[:, 0:P], zeros[:], zeros[:], start=True, stop=True)
+            nc.tensor.matmul(warm_bank[:, 0:P], zeros, zeros, start=True, stop=True)
 
         ctx_rows = keep.tile([P, C], BF16)
         w_rows = [
@@ -106,9 +105,9 @@ def tile_probcrossattention_pa_s_kernel(
             )
 
         load_piece(0)
+        load_piece(1)
         nc.sync.dma_start(out=bias_rows[0:4, :], in_=bk.rearrange("(r c) -> r c", r=4))
         nc.sync.dma_start(out=bias_rows[4:8, :], in_=bv.rearrange("(r c) -> r c", r=4))
-        load_piece(1)
         nc.sync.dma_start(out=ctx_rows[:], in_=context.flatten_outer_dims())
         for b in range(2, 6):
             load_piece(b)
@@ -220,28 +219,32 @@ def tile_probcrossattention_pa_s_kernel(
             )
             return result
 
-        def mean_and_rstd(quarter, name):
-            mean_var = small.tile([P, 2], F32, name=name + "_mean_var")
-            nc.vector.bn_aggr(out=mean_var[:], in_=stats[:, quarter - V_MU, :])
-            rstd = small.tile([P, 1], F32, name=name + "_rstd")
+        mean_var = small.tile([P, 2, 2], F32)
+        rstd = small.tile([P, 2], F32)
+
+        def aggregate(quarter):
+            nc.vector.bn_aggr(out=mean_var[:, quarter - V_MU, :], in_=stats[:, quarter - V_MU, :])
+
+        def reciprocal_roots():
             nc.gpsimd.tensor_scalar(
-                out=rstd[:], in0=mean_var[:, 1:2], scalar1=LN_EPS, scalar2=None, op0=ALU.add
+                out=rstd[:], in0=mean_var[:, :, 1], scalar1=LN_EPS, scalar2=None, op0=ALU.add
             )
             nc.gpsimd.tensor_tensor(out=rstd[:], in0=rstd[:], in1=minus_half[:], op=ALU.pow)
-            return mean_var, rstd
 
-        def centre_and_gain(quarter, mean_var, gain, name):
+        def centre_and_gain(quarter, gain, name):
             centred = keep.tile([P, C], F32, name=name + "_centred")
             nc.vector.scalar_tensor_tensor(
-                out=centred[:], in0=x_all[:, quarter, :], scalar=mean_var[:, 0:1],
+                out=centred[:], in0=x_all[:, quarter, :],
+                scalar=mean_var[:, quarter - V_MU, 0:1],
                 in1=gain, op0=ALU.subtract, op1=ALU.mult,
             )
             return centred
 
-        def scale_and_shift(centred, rstd, shift, name):
+        def scale_and_shift(quarter, centred, shift, name):
             normed = keep.tile([P, C], F32, name=name + "_mu")
             nc.vector.scalar_tensor_tensor(
-                out=normed[:], in0=centred[:], scalar=rstd[:, 0:1], in1=shift,
+                out=normed[:], in0=centred[:],
+                scalar=rstd[:, quarter - V_MU : quarter - V_MU + 1], in1=shift,
                 op0=ALU.mult, op1=ALU.add,
             )
             return normed
@@ -264,16 +267,16 @@ def tile_probcrossattention_pa_s_kernel(
 
         flip(0)
         group(0, "scalar")
-        bias_columns = rows_to_columns(nc, psum, small, bias_rows, 8, ident, "bias_columns")
         flip(1)
         group(1, "scalar")
+        bias_columns = rows_to_columns(nc, psum, small, bias_rows, 8, ident, "bias_columns")
         quantise(0)
-        spread_biases(V_VAR, nc.scalar.copy)
         ctx_bank = flip_context()
         group_context(ctx_bank)
         quantise(1)
         flip(2)
         group(2, "scalar")
+        spread_biases(V_VAR, nc.scalar.copy)
         quantise_context()
         flip(3)
         group(3, "scalar")
@@ -309,19 +312,20 @@ def tile_probcrossattention_pa_s_kernel(
         k_affine = spread_affine(1, "k_affine")
         statistics(V_MU)
         add_bias(K_MU)
-        v_mean_var, v_rstd = mean_and_rstd(V_MU, "v")
+        aggregate(V_MU)
         statistics(K_MU)
-        v_centred = centre_and_gain(V_MU, v_mean_var, v_affine[:, 0:C], "v")
-        k_mean_var, k_rstd = mean_and_rstd(K_MU, "k")
-        v_mu = scale_and_shift(v_centred, v_rstd, v_affine[:, C : 2 * C], "v")
-        k_centred = centre_and_gain(K_MU, k_mean_var, k_affine[:, 0:C], "k")
+        v_centred = centre_and_gain(V_MU, v_affine[:, 0:C], "v")
+        aggregate(K_MU)
+        reciprocal_roots()
+        k_centred = centre_and_gain(K_MU, k_affine[:, 0:C], "k")
         logarithm(V_VAR, math.exp(-VAR_EPS))
         logarithm(K_VAR, math.exp(-VAR_EPS))
         v_var = softplus(V_VAR, "v_var")
-        k_mu = scale_and_shift(k_centred, k_rstd, k_affine[:, C : 2 * C], "k")
-        nc.sync.dma_start(out=k_mu_out, in_=k_mu[:])
         k_var = softplus(K_VAR, "k_var")
         nc.sync.dma_start(out=k_var_out, in_=k_var[:])
+        k_mu = scale_and_shift(K_MU, k_centred, k_affine[:, C : 2 * C], "k")
+        nc.sync.dma_start(out=k_mu_out, in_=k_mu[:])
+        v_mu = scale_and_shift(V_MU, v_centred, v_affine[:, C : 2 * C], "v")
         v_std = keep.tile([P, C], F32)
         spread_noise = keep.tile([P, C], F32)
         v_sample = keep.tile([P, C], F32)

import math
from contextlib import ExitStack

import concourse.mybir as mybir
from concourse.masks import make_identity

F32 = mybir.dt.float32
BF16 = mybir.dt.bfloat16
U32 = mybir.dt.uint32
U8 = mybir.dt.uint8
FP8X4 = mybir.dt.float8_e4m3fn_x4
ALU = mybir.AluOpType
ACT = mybir.ActivationFunctionType

P = 128
C = 512
BANK = 512
V_VAR, K_VAR, V_MU, K_MU = 0, 1, 2, 3
PIECES = ((V_VAR, 0, 128), (V_VAR, 128, 128), (V_VAR, 256, 256)) + tuple(
    (quarter, first, 256) for quarter in (K_VAR, V_MU, K_MU) for first in (0, 256)
)
VAR_EPS = 1e-6
LN_EPS = 1e-5
TINY = 1e-36
WARM_UPS = 3

FLOPS = 2 * P * C * 4 * C


def transpose_words(nc, bank, first_column, rows_bf16, ident):
    words = rows_bf16.bitcast(F32)
    for u in range(2):
        nc.tensor.transpose(
            bank[:, first_column + P * u : first_column + P * (u + 1)],
            words[:, u : 2 * P : 2],
            ident[:],
        )


def rows_to_columns(nc, psum, small, rows, n_rows, ident, name):
    flipped = psum.tile([P, BANK], F32, tag="words", name=name + "_flipped")
    nc.tensor.transpose(flipped[:, 0:P], rows[:].bitcast(F32), ident[:])
    columns = small.tile([P, n_rows], F32, name=name)
    nc.vector.tensor_copy(out=columns[:], in_=flipped[:, 0:n_rows])
    return columns


def repeat_on_all_partitions(nc, bank, columns, four_rows, ident):
    for i, r in enumerate(four_rows):
        nc.tensor.transpose(
            bank[:, P * i : P * (i + 1)], columns[:, r : r + 1].to_broadcast([P, P]), ident[:]
        )


def tile_probcrossattention_pa_s_kernel(
    tc, context, eps_noise, Wk, bk, Wv, bv, ln_k_g, ln_k_b, ln_v_g, ln_v_b, out_0, out_1, out_2
):
    nc = tc.nc
    k_mu_out = out_0.flatten_outer_dims()
    k_var_out = out_1.flatten_outer_dims()
    v_sample_out = out_2.flatten_outer_dims()

    quarter_weights = (Wv, Wk, Wv, Wk)
    quarter_first_row = (C, C, 0, 0)
    quarter_bias_row = (6, 2, 4, 0)

    with ExitStack() as stack:
        stack.enter_context(tc.manual_schedule())
        keep = stack.enter_context(tc.tile_pool(name="keep", bufs=1))
        small = stack.enter_context(tc.tile_pool(name="small", bufs=1))
        psum = stack.enter_context(tc.psum_pool(name="psum", bufs=4))
        psum_acc = stack.enter_context(tc.psum_pool(name="psum_acc", bufs=2))
        psum_affine = stack.enter_context(tc.psum_pool(name="psum_affine", bufs=1))

        bias_rows = keep.tile([P, 2 * P], BF16)
        nc.vector.memset(bias_rows[:].bitcast(F32), 0.0)
        affine_rows = keep.tile([P, 2 * P], BF16)
        nc.vector.memset(affine_rows[:].bitcast(F32), 0.0)
        ident = keep.tile([P, P], F32)
        make_identity(nc, ident[:])
        minus_half = small.tile([P, 2], F32)
        nc.vector.memset(minus_half[:], -0.5)
        warm = small.tile([P, 1], F32)
        nc.scalar.activation(out=warm[:], in_=minus_half[:, 0:1], func=ACT.Sigmoid)

        zeros = affine_rows[:].bitcast(F32)
        warm_bank = psum.tile([P, BANK], F32, tag="words", name="warm_bank")
        for i in range(WARM_UPS):
            nc.tensor.matmul(warm_bank[:, 0:P], zeros, zeros, start=True, stop=True)

        ctx_rows = keep.tile([P, C], BF16)
        w_rows = [
            keep.tile([P, rows // P, C], BF16, name="w_rows%d" % b)
            for b, (quarter, first, rows) in enumerate(PIECES)
        ]

        def load_piece(b):
            quarter, first, rows = PIECES[b]
            first_row = quarter_first_row[quarter] + first
            nc.sync.dma_start(
                out=w_rows[b][:],
                in_=quarter_weights[quarter][first_row : first_row + rows, :].rearrange(
                    "(p t) k -> p t k", p=P
                ),
            )

        load_piece(0)
        load_piece(1)
        nc.sync.dma_start(out=bias_rows[0:4, :], in_=bk.rearrange("(r c) -> r c", r=4))
        nc.sync.dma_start(out=bias_rows[4:8, :], in_=bv.rearrange("(r c) -> r c", r=4))
        nc.sync.dma_start(out=ctx_rows[:], in_=context.flatten_outer_dims())
        for b in range(2, 6):
            load_piece(b)
        for i, vector in enumerate((ln_v_g, ln_v_b, ln_k_g, ln_k_b)):
            nc.sync.dma_start(
                out=affine_rows[2 * i : 2 * i + 2, :], in_=vector.rearrange("(r c) -> r c", r=2)
            )
        for b in range(6, len(PIECES)):
            load_piece(b)
        noise = keep.tile([P, C], BF16)
        nc.sync.dma_start(out=noise[:], in_=eps_noise.flatten_outer_dims())

        ctx_grouped = keep.tile([P, 4 * P], BF16, align_bytes=64)
        ctx_codes = keep.tile([P, P], U32, align_bytes=64)
        ctx_scales = keep.tile([P, P], U8, align_bytes=64)
        grouped = [
            keep.tile([P, 4 * rows], BF16, align_bytes=64, name="grouped%d" % b)
            for b, (quarter, first, rows) in enumerate(PIECES)
        ]
        w_codes = keep.tile([P, 4, C], U32, align_bytes=64)
        w_scales = keep.tile([P, 4, C], U8, align_bytes=64)
        x_all = keep.tile([P, 4, C], F32)
        sig = keep.tile([P, 2, C], F32)
        log_term = keep.tile([P, 2, C], F32)
        bias_all = keep.tile([P, 4, C], BF16)
        stats = small.tile([P, 2, 6], F32)
        banks = {}
        accs = {}

        def flip(b):
            bank = psum.tile([P, BANK], F32, tag="words", name="w_bank%d" % b)
            for t in range(PIECES[b][2] // P):
                transpose_words(nc, bank, 2 * P * t, w_rows[b][:, t, :], ident)
            banks[b] = bank

        def group(b, engine):
            rows = PIECES[b][2]
            source = banks[b][:, 0 : 2 * rows].rearrange("p (t u n) -> p n t u", u=2, n=P)
            target = grouped[b][:].bitcast(F32).rearrange("p (n t u) -> p n t u", u=2, n=P)
            if engine == "scalar":
                nc.scalar.copy(out=target, in_=source)
            else:
                nc.vector.tensor_copy(out=target, in_=source)

        def quantise(b):
            quarter, first, rows = PIECES[b]
            cols = slice(first, first + rows)
            nc.vector.quantize_mx(
                out=w_codes[:, quarter, cols].bitcast(FP8X4),
                scales=w_scales[:, quarter, cols],
                in_=grouped[b][:],
            )

        def multiply(quarter):
            acc = psum_acc.tile([P, C], F32, name="acc")
            nc.tensor.matmul_mx(
                out=acc[:],
                lhsT=ctx_codes[:].bitcast(FP8X4),
                lhsT_scale=ctx_scales[:],
                rhs=w_codes[:, quarter, :].bitcast(FP8X4),
                rhs_scale=w_scales[:, quarter, :],
                start=True,
                stop=True,
            )
            accs[quarter] = acc

        def add_bias(quarter):
            nc.vector.tensor_tensor(
                out=x_all[:, quarter, :], in0=accs[quarter][:], in1=bias_all[:, quarter, :], op=ALU.add
            )

        def spread_biases(first_quarter, copy):
            four_rows = []
            for quarter in (first_quarter, first_quarter + 1):
                four_rows.extend((quarter_bias_row[quarter], quarter_bias_row[quarter] + 1))
            bank = psum.tile([P, BANK], F32, tag="words", name="bias_bank%d" % first_quarter)
            repeat_on_all_partitions(nc, bank, bias_columns, four_rows, ident)
            copy(
                out=bias_all[:, first_quarter : first_quarter + 2, :]
                .rearrange("p q c -> p (q c)")
                .bitcast(F32),
                in_=bank[:],
            )

        def spread_affine(i, name):
            bank = psum_affine.tile([P, BANK], F32, name=name)
            repeat_on_all_partitions(nc, bank, affine_columns, range(4 * i, 4 * i + 4), ident)
            return bank[:].bitcast(BF16)

        def statistics(quarter):
            nc.vector.bn_stats(out=stats[:, quarter - V_MU, :], in_=x_all[:, quarter, :])

        def sigmoid(quarter):
            nc.scalar.activation(
                out=sig[:, quarter, :], in_=x_all[:, quarter, :], func=ACT.Sigmoid, scale=-1.0
            )

        def logarithm(quarter, scale):
            nc.scalar.activation(
                out=log_term[:, quarter, :], in_=sig[:, quarter, :], func=ACT.Ln, bias=TINY,
                scale=scale,
            )

        def softplus(quarter, name):
            result = keep.tile([P, C], F32, name=name)
            nc.vector.scalar_tensor_tensor(
                out=result[:], in0=log_term[:, quarter, :], scalar=-1.0, in1=x_all[:, quarter, :],
                op0=ALU.mult, op1=ALU.max,
            )
            return result

        mean_var = small.tile([P, 2, 2], F32)
        rstd = small.tile([P, 2], F32)

        def aggregate(quarter):
            nc.vector.bn_aggr(out=mean_var[:, quarter - V_MU, :], in_=stats[:, quarter - V_MU, :])

        def reciprocal_roots():
            nc.gpsimd.tensor_scalar(
                out=rstd[:], in0=mean_var[:, :, 1], scalar1=LN_EPS, scalar2=None, op0=ALU.add
            )
            nc.gpsimd.tensor_tensor(out=rstd[:], in0=rstd[:], in1=minus_half[:], op=ALU.pow)

        def centre_and_gain(quarter, gain, name):
            centred = keep.tile([P, C], F32, name=name + "_centred")
            nc.vector.scalar_tensor_tensor(
                out=centred[:], in0=x_all[:, quarter, :],
                scalar=mean_var[:, quarter - V_MU, 0:1],
                in1=gain, op0=ALU.subtract, op1=ALU.mult,
            )
            return centred

        def scale_and_shift(quarter, centred, shift, name):
            normed = keep.tile([P, C], F32, name=name + "_mu")
            nc.vector.scalar_tensor_tensor(
                out=normed[:], in0=centred[:],
                scalar=rstd[:, quarter - V_MU : quarter - V_MU + 1], in1=shift,
                op0=ALU.mult, op1=ALU.add,
            )
            return normed

        def flip_context():
            bank = psum.tile([P, BANK], F32, tag="words", name="ctx_bank")
            transpose_words(nc, bank, 0, ctx_rows[:], ident)
            return bank

        def group_context(bank):
            nc.vector.tensor_copy(
                out=ctx_grouped[:].bitcast(F32).rearrange("p (n u) -> p n u", u=2),
                in_=bank[:, 0 : 2 * P].rearrange("p (u n) -> p n u", u=2),
            )

        def quantise_context():
            nc.vector.quantize_mx(
                out=ctx_codes[:].bitcast(FP8X4), scales=ctx_scales[:], in_=ctx_grouped[:]
            )

        flip(0)
        group(0, "scalar")
        flip(1)
        group(1, "scalar")
        bias_columns = rows_to_columns(nc, psum, small, bias_rows, 8, ident, "bias_columns")
        quantise(0)
        ctx_bank = flip_context()
        group_context(ctx_bank)
        quantise(1)
        flip(2)
        group(2, "scalar")
        spread_biases(V_VAR, nc.scalar.copy)
        quantise_context()
        flip(3)
        group(3, "scalar")
        quantise(2)
        flip(4)
        group(4, "scalar")
        flip(5)
        group(5, "scalar")
        quantise(3)
        affine_columns = rows_to_columns(nc, psum, small, affine_rows, 8, ident, "affine_columns")
        multiply(V_VAR)
        add_bias(V_VAR)
        flip(6)
        group(6, "scalar")
        quantise(4)
        flip(7)
        group(7, "scalar")
        quantise(5)
        spread_biases(V_MU, nc.scalar.copy)
        multiply(K_VAR)
        quantise(6)
        add_bias(K_VAR)
        flip(8)
        group(8, "scalar")
        multiply(V_MU)
        quantise(7)
        v_affine = spread_affine(0, "v_affine")
        sigmoid(V_VAR)
        sigmoid(K_VAR)
        add_bias(V_MU)
        quantise(8)
        multiply(K_MU)
        k_affine = spread_affine(1, "k_affine")
        statistics(V_MU)
        add_bias(K_MU)
        aggregate(V_MU)
        statistics(K_MU)
        v_centred = centre_and_gain(V_MU, v_affine[:, 0:C], "v")
        aggregate(K_MU)
        reciprocal_roots()
        k_centred = centre_and_gain(K_MU, k_affine[:, 0:C], "k")
        logarithm(V_VAR, math.exp(-VAR_EPS))
        logarithm(K_VAR, math.exp(-VAR_EPS))
        v_var = softplus(V_VAR, "v_var")
        k_var = softplus(K_VAR, "k_var")
        nc.sync.dma_start(out=k_var_out, in_=k_var[:])
        k_mu = scale_and_shift(K_MU, k_centred, k_affine[:, C : 2 * C], "k")
        nc.sync.dma_start(out=k_mu_out, in_=k_mu[:])
        v_mu = scale_and_shift(V_MU, v_centred, v_affine[:, C : 2 * C], "v")
        v_std = keep.tile([P, C], F32)
        spread_noise = keep.tile([P, C], F32)
        v_sample = keep.tile([P, C], F32)
        halves = (slice(0, C // 2), slice(C // 2, C))
        for cols in halves:
            nc.scalar.activation(out=v_std[:, cols], in_=v_var[:, cols], func=ACT.Sqrt)
            nc.vector.tensor_tensor(
                out=spread_noise[:, cols], in0=v_std[:, cols], in1=noise[:, cols], op=ALU.mult
            )
        for cols in halves:
            nc.vector.tensor_tensor(
                out=v_sample[:, cols], in0=spread_noise[:, cols], in1=v_mu[:, cols], op=ALU.add
            )
            nc.sync.dma_start(out=v_sample_out[:, cols], in_=v_sample[:, cols])
